import numpy as np
import ml_dtypes


def mxq(x, axis, fmt="e4m3"):
    dtype, down = {"e4m3": (ml_dtypes.float8_e4m3fn, 7), "e5m2": (ml_dtypes.float8_e5m2, 14)}[fmt]
    v = np.moveaxis(np.asarray(x, np.float32).astype(ml_dtypes.bfloat16).astype(np.float64), axis, -1)
    blocks = v.reshape(v.shape[:-1] + (-1, 32))
    amax = np.abs(blocks).max(-1, keepdims=True)
    byte = np.maximum(np.where(amax > 0, np.frexp(amax)[1] - 1 + 127, 0) - down, 1)
    scale = np.exp2(byte - 127.0)
    codes = (blocks / scale).astype(np.float32).astype(dtype).astype(np.float64)
    return np.moveaxis((codes * scale).reshape(v.shape), -1, axis)


WIDE = False


def mx_kscale(k):
    if not WIDE:
        return np.ones(k)
    levels = np.array([10, -10, 5, -5, 0])
    a = np.random.permutation(np.resize(levels, k // 512 * 4)).reshape(k // 512, 4)
    idx = np.arange(k)
    return np.exp2(a[idx // 512, idx % 128 // 32])


BF16 = ml_dtypes.bfloat16


def bf(x):
    return np.asarray(x, np.float32).astype(BF16)


def f64(x):
    return np.asarray(x).astype(np.float64)


B, N, D, H, HD, FF = 8, 1024, 1024, 2, 64, 4096
E = H * HD
EPS = 1e-5


def layernorm(x, gamma, beta):
    mu = x.mean(-1, keepdims=True)
    var = ((x - mu) ** 2).mean(-1, keepdims=True)
    return (x - mu) * (1.0 / np.sqrt(var + EPS)) * gamma + beta


def heads(y):
    return y.reshape(B, N, H, HD).transpose(0, 2, 1, 3)


def setup_inputs():
    s = mx_kscale(D)
    r = np.random.standard_normal
    return {"x": bf(r((B, N, D))),
            "gamma": bf((1.0 + 0.1 * r(D)) * s), "beta": bf(0.1 * r(D) * s),
            "Wq": bf(r((D, E)) * 1.4 / np.sqrt(D) / s[:, None]), "bq": bf(r(E) * 0.2),
            "Wk": bf(r((D, E)) * 1.4 / np.sqrt(D) / s[:, None]), "bk": bf(r(E) * 0.2),
            "Wv": bf(r((D, E)) * 1.0 / np.sqrt(D) / s[:, None]), "bv": bf(r(E) * 0.2)}


def reference(x, gamma, beta, Wq, bq, Wk, bk, Wv, bv):
    h = layernorm(f64(x), f64(gamma), f64(beta))
    hq = mxq(h, 2, "e4m3")
    q = (hq @ mxq(f64(Wq), 0, "e4m3")) + f64(bq)
    k = (hq @ mxq(f64(Wk), 0, "e4m3")) + f64(bk)
    v = (hq @ mxq(f64(Wv), 0, "e4m3")) + f64(bv)
    return heads(q), heads(k), heads(v)

@@ -1,0 +1,212 @@
+from contextlib import ExitStack
+
+import concourse.mybir as mybir
+from concourse.masks import make_identity
+
+F32 = mybir.dt.float32
+BF16 = mybir.dt.bfloat16
+U32 = mybir.dt.uint32
+U8 = mybir.dt.uint8
+FP8X4 = mybir.dt.float8_e4m3fn_x4
+ALU = mybir.AluOpType
+ACTF = mybir.ActivationFunctionType
+
+P = 128
+ROWS = 8192
+D = 1024
+E = 128
+NOUT = 3 * E
+JT = 4
+GROUP = P * JT
+NG = ROWS // GROUP
+KT = D // P
+PASSES = 2
+EPS = 1e-5
+FLOPS = 2 * ROWS * D * NOUT
+
+RV = 64
+
+
+def tile_vit_transformerblock_pa_t_kernel(
+    tc, x, gamma, beta, Wq, bq, Wk, bk, Wv, bv, out_0, out_1, out_2
+):
+    nc = tc.nc
+    outs = [out_0, out_1, out_2]
+    with ExitStack() as ctx:
+        const = ctx.enter_context(tc.tile_pool(name="const", bufs=1))
+        xpool = ctx.enter_context(tc.tile_pool(name="xpool", bufs=5))
+        small = ctx.enter_context(tc.tile_pool(name="small", bufs=4))
+        xnpool = ctx.enter_context(tc.tile_pool(name="xnpool", bufs=2))
+        hpool = ctx.enter_context(tc.tile_pool(name="hpool", bufs=3))
+        qpool = ctx.enter_context(tc.tile_pool(name="qpool", bufs=3))
+        opool = ctx.enter_context(tc.tile_pool(name="opool", bufs=3))
+        tpsum = ctx.enter_context(tc.psum_pool(name="tpsum", bufs=6))
+        mpsum = ctx.enter_context(tc.psum_pool(name="mpsum", bufs=2))
+
+        xg = x.flatten_outer_dims().rearrange("(g p j) k -> g p (j k)", p=P, j=JT)
+
+        xts = {}
+
+        def load(i):
+            xt = xpool.tile([P, JT, D], BF16)
+            nc.sync.dma_start(out=xt[:].rearrange("p j k -> p (j k)"), in_=xg[i])
+            xts[i] = xt
+
+        load(0)
+        load(1)
+
+        ident = const.tile([P, P], F32)
+        make_identity(nc, ident[:])
+        eps = const.tile([P, 1], F32)
+        nc.vector.memset(eps[:], EPS)
+
+        gb = const.tile([P, P], BF16)
+        nc.vector.memset(gb[:], 0.0)
+        nc.scalar.dma_start(out=gb[0:KT, :], in_=gamma.rearrange("(c p) -> c p", p=P))
+        nc.scalar.dma_start(out=gb[KT : 2 * KT, :], in_=beta.rearrange("(c p) -> c p", p=P))
+        gbf = const.tile([P, P], F32)
+        nc.vector.tensor_copy(out=gbf[:], in_=gb[:])
+        gbp = tpsum.tile([P, 512], F32, tag="tp")
+        nc.tensor.transpose(gbp[:, 0:P], gbf[:], ident[:])
+        gbc = const.tile([P, 2 * KT], F32)
+        nc.vector.tensor_copy(out=gbc[:], in_=gbp[:, 0 : 2 * KT])
+
+        wraw = const.tile([P, KT, NOUT], BF16)
+        for s, w in enumerate([Wq, Wk, Wv]):
+            nc.scalar.dma_start(
+                out=wraw[:, :, s * E : (s + 1) * E],
+                in_=w.rearrange("(c p) n -> p c n", p=P),
+            )
+        wgrp = const.tile([P, PASSES, 512, 4], BF16, align_bytes=64)
+        nc.vector.memset(wgrp[:, :, NOUT:512, :], 0.0)
+        for g in range(PASSES):
+            nc.vector.tensor_copy(
+                out=wgrp[:, g, 0:NOUT, :],
+                in_=wraw[:, 4 * g : 4 * g + 4, :].rearrange("p t n -> p n t"),
+            )
+        wc = const.tile([P, PASSES * 512], U32, align_bytes=64)
+        wsc = const.tile([P, PASSES * 512], U8, align_bytes=64)
+        nc.vector.quantize_mx(
+            out=wc[:].bitcast(FP8X4),
+            scales=wsc[:],
+            in_=wgrp[:].rearrange("p g n t -> p (g n t)"),
+        )
+
+        bb = const.tile([P, NOUT], BF16)
+        for s, b in enumerate([bq, bk, bv]):
+            nc.scalar.dma_start(out=bb[:, s * E : (s + 1) * E], in_=b.partition_broadcast(P))
+        bias = const.tile([P, NOUT], F32)
+        nc.vector.tensor_copy(out=bias[:], in_=bb[:])
+
+        stats_of = {}
+        xns = {}
+        cods = {}
+
+        def stats(i):
+            xt = xts[i]
+            st = small.tile([P, JT, 2, 6], F32)
+            for j in range(JT):
+                for c in range(2):
+                    nc.vector.bn_stats(out=st[:, j, c, :], in_=xt[:, j, c * 512 : (c + 1) * 512])
+            mv = small.tile([P, JT, 2], F32)
+            for j in range(JT):
+                nc.vector.bn_aggr(out=mv[:, j, :], in_=st[:, j, :, :].rearrange("p c s -> p (c s)"))
+            sd = small.tile([P, JT], F32)
+            nc.scalar.activation(out=sd[:], in_=mv[:, :, 1], func=ACTF.Sqrt, bias=eps[:, 0:1], scale=1.0)
+            rs = small.tile([P, JT], F32)
+            nc.vector.reciprocal(out=rs[:], in_=sd[:])
+            nm = small.tile([P, JT], F32)
+            nc.vector.tensor_scalar(out=nm[:], in0=mv[:, :, 0], scalar1=-1.0, scalar2=None, op0=ALU.mult)
+            stats_of[i] = (nm, rs)
+
+        def norm(i):
+            xt = xts[i]
+            nm, rs = stats_of[i]
+            xn = xnpool.tile([P, JT, D], F32)
+            for j in range(JT):
+                nc.gpsimd.tensor_scalar(
+                    out=xn[:, j, :],
+                    in0=xt[:, j, :],
+                    scalar1=nm[:, j : j + 1],
+                    scalar2=rs[:, j : j + 1],
+                    op0=ALU.add,
+                    op1=ALU.mult,
+                )
+            xns[i] = xn
+
+        def quantise(i):
+            xn = xns[i]
+            cod = qpool.tile([P, PASSES, 512], U32, align_bytes=64)
+            sc = qpool.tile([P, PASSES, 512], U8, align_bytes=64)
+            for g in range(PASSES):
+                hp = hpool.tile([P, 4, 512], BF16)
+                for t in range(4):
+                    kt = 4 * g + t
+                    tp = tpsum.tile([P, 512], F32, tag="tp")
+                    for j in range(JT):
+                        nc.tensor.transpose(
+                            tp[:, j * P : (j + 1) * P], xn[:, j, kt * P : (kt + 1) * P], ident[:]
+                        )
+                    nc.scalar.activation(
+                        out=hp[:, t, :],
+                        in_=tp[:],
+                        func=ACTF.Identity,
+                        bias=gbc[:, KT + kt : KT + kt + 1],
+                        scale=gbc[:, kt : kt + 1],
+                    )
+                grp = hpool.tile([P, 512, 4], BF16, align_bytes=64)
+                nc.vector.tensor_copy(
+                    out=grp[:, 0:RV, :].rearrange("p (c i) t -> p c t i", i=4),
+                    in_=hp[:, :, 0:RV].rearrange("p t (c i) -> p c t i", i=4),
+                )
+                nc.scalar.copy(
+                    out=grp[:, RV:512, :].rearrange("p (c i) t -> p c t i", i=4),
+                    in_=hp[:, :, RV:512].rearrange("p t (c i) -> p c t i", i=4),
+                )
+                nc.vector.quantize_mx(
+                    out=cod[:, g, :].bitcast(FP8X4),
+                    scales=sc[:, g, :],
+                    in_=grp[:].rearrange("p c t -> p (c t)"),
+                )
+            cods[i] = (cod, sc)
+
+        def project(i):
+            cod, sc = cods[i]
+            ot = opool.tile([P, 6, JT, 64], F32)
+            for j in range(JT):
+                ps = mpsum.tile([P, 512], F32, tag="mm")
+                for c0, cw in ((0, 256), (256, 128)):
+                    for g in range(PASSES):
+                        nc.tensor.matmul_mx(
+                            out=ps[:, c0 : c0 + cw],
+                            lhsT=cod[:, g, j * P : (j + 1) * P].bitcast(FP8X4),
+                            lhsT_scale=sc[:, g, j * P : (j + 1) * P],
+                            rhs=wc[:, g * 512 + c0 : g * 512 + c0 + cw].bitcast(FP8X4),
+                            rhs_scale=wsc[:, g * 512 + c0 : g * 512 + c0 + cw],
+                            start=(g == 0),
+                            stop=(g == PASSES - 1),
+                        )
+                nc.vector.tensor_tensor(
+                    out=ot[:, :, j, :],
+                    in0=ps[:, 0:NOUT].rearrange("p (c d) -> p c d", d=64),
+                    in1=bias[:].rearrange("p (c d) -> p c d", d=64),
+                    op=ALU.add,
+                )
+            b, half = divmod(i, 2)
+            for s in range(3):
+                dst = outs[s][b].rearrange("a (h p j) d -> h p a (j d)", h=2, p=P, j=JT)[half]
+                nc.sync.dma_start(
+                    out=dst, in_=ot[:, 2 * s : 2 * s + 2, :, :].rearrange("p a j d -> p a (j d)")
+                )
+
+        for i in range(-2, NG + 1):
+            if 0 <= i + 4 < NG and i + 4 >= 2:
+                load(i + 4)
+            if 0 <= i + 2 < NG:
+                stats(i + 2)
+            if 0 <= i + 1 < NG:
+                norm(i + 1)
+            if 0 <= i < NG:
+                quantise(i)
+            if 0 <= i - 1 < NG:
+                project(i - 1)

@@ -19,12 +19,24 @@ NOUT = 3 * E
 JT = 4
 GROUP = P * JT
 NG = ROWS // GROUP
+NU = 2 * NG
 KT = D // P
 PASSES = 2
 EPS = 1e-5
 FLOPS = 2 * ROWS * D * NOUT
 
-RV = 64
+LOAD_LEAD = 5
+XBUFS = 10
+TPB = 5
+SWITCH = 22
+RV_EARLY = 0
+RV_LATE = 448
+PRE = 3
+EXTRA = 2
+
+
+def rv_cols(u):
+    return RV_EARLY if u < SWITCH else RV_LATE
 
 
 def tile_vit_transformerblock_pa_t_kernel(
@@ -34,151 +46,209 @@ def tile_vit_transformerblock_pa_t_kernel(
     outs = [out_0, out_1, out_2]
     with ExitStack() as ctx:
         const = ctx.enter_context(tc.tile_pool(name="const", bufs=1))
-        xpool = ctx.enter_context(tc.tile_pool(name="xpool", bufs=5))
-        small = ctx.enter_context(tc.tile_pool(name="small", bufs=4))
+        xpool = ctx.enter_context(tc.tile_pool(name="xpool", bufs=XBUFS))
+        small = ctx.enter_context(tc.tile_pool(name="small", bufs=8))
         xnpool = ctx.enter_context(tc.tile_pool(name="xnpool", bufs=2))
         hpool = ctx.enter_context(tc.tile_pool(name="hpool", bufs=3))
         qpool = ctx.enter_context(tc.tile_pool(name="qpool", bufs=3))
         opool = ctx.enter_context(tc.tile_pool(name="opool", bufs=3))
-        tpsum = ctx.enter_context(tc.psum_pool(name="tpsum", bufs=6))
-        mpsum = ctx.enter_context(tc.psum_pool(name="mpsum", bufs=2))
+        tpsum = ctx.enter_context(tc.psum_pool(name="tpsum", bufs=TPB))
+        mpsum = ctx.enter_context(tc.psum_pool(name="mpsum", bufs=8 - TPB))
+        ctx.enter_context(tc.manual_schedule())
 
-        xg = x.flatten_outer_dims().rearrange("(g p j) k -> g p (j k)", p=P, j=JT)
+        xg = x.flatten_outer_dims().rearrange("(g p j) k -> g p j k", p=P, j=JT)
 
         xts = {}
+        sts = {}
+        sds = {}
+        fins = {}
+        xns = {}
+        tps = {}
+        hps = {}
+        grps = {}
+        cods = {}
+        pss = {}
+        ots = {}
 
-        def load(i):
+        def load(i, parts):
             xt = xpool.tile([P, JT, D], BF16)
-            nc.sync.dma_start(out=xt[:].rearrange("p j k -> p (j k)"), in_=xg[i])
+            step = JT // parts
+            for a in range(parts):
+                nc.sync.dma_start(
+                    out=xt[:, a * step : (a + 1) * step, :], in_=xg[i][:, a * step : (a + 1) * step, :]
+                )
             xts[i] = xt
-
-        load(0)
-        load(1)
-
-        ident = const.tile([P, P], F32)
-        make_identity(nc, ident[:])
-        eps = const.tile([P, 1], F32)
-        nc.vector.memset(eps[:], EPS)
 
         gb = const.tile([P, P], BF16)
         nc.vector.memset(gb[:], 0.0)
         nc.scalar.dma_start(out=gb[0:KT, :], in_=gamma.rearrange("(c p) -> c p", p=P))
         nc.scalar.dma_start(out=gb[KT : 2 * KT, :], in_=beta.rearrange("(c p) -> c p", p=P))
-        gbf = const.tile([P, P], F32)
-        nc.vector.tensor_copy(out=gbf[:], in_=gb[:])
-        gbp = tpsum.tile([P, 512], F32, tag="tp")
-        nc.tensor.transpose(gbp[:, 0:P], gbf[:], ident[:])
-        gbc = const.tile([P, 2 * KT], F32)
-        nc.vector.tensor_copy(out=gbc[:], in_=gbp[:, 0 : 2 * KT])
-
+        load(0, 4)
+        load(1, 1)
         wraw = const.tile([P, KT, NOUT], BF16)
         for s, w in enumerate([Wq, Wk, Wv]):
-            nc.scalar.dma_start(
+            nc.sync.dma_start(
                 out=wraw[:, :, s * E : (s + 1) * E],
                 in_=w.rearrange("(c p) n -> p c n", p=P),
             )
-        wgrp = const.tile([P, PASSES, 512, 4], BF16, align_bytes=64)
-        nc.vector.memset(wgrp[:, :, NOUT:512, :], 0.0)
-        for g in range(PASSES):
-            nc.vector.tensor_copy(
-                out=wgrp[:, g, 0:NOUT, :],
-                in_=wraw[:, 4 * g : 4 * g + 4, :].rearrange("p t n -> p n t"),
-            )
-        wc = const.tile([P, PASSES * 512], U32, align_bytes=64)
-        wsc = const.tile([P, PASSES * 512], U8, align_bytes=64)
-        nc.vector.quantize_mx(
-            out=wc[:].bitcast(FP8X4),
-            scales=wsc[:],
-            in_=wgrp[:].rearrange("p g n t -> p (g n t)"),
-        )
-
+        for i in range(2, LOAD_LEAD):
+            load(i, 1)
         bb = const.tile([P, NOUT], BF16)
         for s, b in enumerate([bq, bk, bv]):
-            nc.scalar.dma_start(out=bb[:, s * E : (s + 1) * E], in_=b.partition_broadcast(P))
+            nc.sync.dma_start(out=bb[:, s * E : (s + 1) * E], in_=b.partition_broadcast(P))
+        loaded = [LOAD_LEAD]
+
+        ident = const.tile([P, P], F32)
+        make_identity(nc, ident[:])
+        eps = const.tile([P, 1], F32)
+        nc.vector.memset(eps[:], EPS)
+        wgrp = const.tile([P, PASSES, 512, 4], BF16, align_bytes=64)
+        nc.vector.memset(wgrp[:, :, NOUT:512, :], 0.0)
+        gbc = const.tile([P, 2 * KT], F32)
+        wc = const.tile([P, PASSES * 512], U32, align_bytes=64)
+        wsc = const.tile([P, PASSES * 512], U8, align_bytes=64)
         bias = const.tile([P, NOUT], F32)
-        nc.vector.tensor_copy(out=bias[:], in_=bb[:])
 
-        stats_of = {}
-        xns = {}
-        cods = {}
+        def prep_gamma():
+            gbf = const.tile([P, P], F32)
+            nc.vector.tensor_copy(out=gbf[:], in_=gb[:])
+            gbp = tpsum.tile([P, 512], F32, tag="tp")
+            nc.tensor.transpose(gbp[:, 0:P], gbf[:], ident[:])
+            nc.vector.tensor_copy(out=gbc[:], in_=gbp[:, 0 : 2 * KT])
 
-        def stats(i):
-            xt = xts[i]
-            st = small.tile([P, JT, 2, 6], F32)
-            for j in range(JT):
-                for c in range(2):
-                    nc.vector.bn_stats(out=st[:, j, c, :], in_=xt[:, j, c * 512 : (c + 1) * 512])
-            mv = small.tile([P, JT, 2], F32)
-            for j in range(JT):
-                nc.vector.bn_aggr(out=mv[:, j, :], in_=st[:, j, :, :].rearrange("p c s -> p (c s)"))
-            sd = small.tile([P, JT], F32)
-            nc.scalar.activation(out=sd[:], in_=mv[:, :, 1], func=ACTF.Sqrt, bias=eps[:, 0:1], scale=1.0)
-            rs = small.tile([P, JT], F32)
-            nc.vector.reciprocal(out=rs[:], in_=sd[:])
-            nm = small.tile([P, JT], F32)
-            nc.vector.tensor_scalar(out=nm[:], in0=mv[:, :, 0], scalar1=-1.0, scalar2=None, op0=ALU.mult)
-            stats_of[i] = (nm, rs)
+        def w_regroup(g):
+            nc.gpsimd.tensor_scalar(
+                out=wgrp[:, g, 0:NOUT, :],
+                in0=wraw[:, 4 * g : 4 * g + 4, :].rearrange("p t n -> p n t"),
+                scalar1=1.0,
+                scalar2=0.0,
+                op0=ALU.mult,
+                op1=ALU.add,
+            )
 
-        def norm(i):
-            xt = xts[i]
-            nm, rs = stats_of[i]
-            xn = xnpool.tile([P, JT, D], F32)
-            for j in range(JT):
-                nc.gpsimd.tensor_scalar(
-                    out=xn[:, j, :],
-                    in0=xt[:, j, :],
-                    scalar1=nm[:, j : j + 1],
-                    scalar2=rs[:, j : j + 1],
-                    op0=ALU.add,
-                    op1=ALU.mult,
-                )
-            xns[i] = xn
+        def bias_cast():
+            nc.gpsimd.tensor_scalar(
+                out=bias[:], in0=bb[:], scalar1=1.0, scalar2=0.0, op0=ALU.mult, op1=ALU.add
+            )
 
-        def quantise(i):
-            xn = xns[i]
-            cod = qpool.tile([P, PASSES, 512], U32, align_bytes=64)
-            sc = qpool.tile([P, PASSES, 512], U8, align_bytes=64)
-            for g in range(PASSES):
-                hp = hpool.tile([P, 4, 512], BF16)
-                for t in range(4):
-                    kt = 4 * g + t
-                    tp = tpsum.tile([P, 512], F32, tag="tp")
-                    for j in range(JT):
-                        nc.tensor.transpose(
-                            tp[:, j * P : (j + 1) * P], xn[:, j, kt * P : (kt + 1) * P], ident[:]
-                        )
-                    nc.scalar.activation(
-                        out=hp[:, t, :],
-                        in_=tp[:],
-                        func=ACTF.Identity,
-                        bias=gbc[:, KT + kt : KT + kt + 1],
-                        scale=gbc[:, kt : kt + 1],
+        def w_quant():
+            nc.vector.quantize_mx(
+                out=wc[:].bitcast(FP8X4),
+                scales=wsc[:],
+                in_=wgrp[:].rearrange("p g n t -> p (g n t)"),
+            )
+
+        def bn(i, j):
+            if j == 0:
+                st = small.tile([P, JT, 2, 6], F32)
+                mv = small.tile([P, JT, 2], F32)
+                sd = small.tile([P, JT], F32)
+                rs = small.tile([P, JT], F32)
+                nm = small.tile([P, JT], F32)
+                sts[i] = (st, mv, sd, rs, nm)
+            st = sts[i][0]
+            mv = sts[i][1]
+            for c in range(2):
+                nc.vector.bn_stats(out=st[:, j, c, :], in_=xts[i][:, j, c * 512 : (c + 1) * 512])
+            nc.vector.bn_aggr(out=mv[:, j, :], in_=st[:, j, :, :].rearrange("p c s -> p (c s)"))
+
+        def root(i, j0, j1):
+            mv = sts[i][1]
+            sd = sts[i][2]
+            nc.scalar.activation(
+                out=sd[:, j0:j1], in_=mv[:, j0:j1, 1], func=ACTF.Sqrt, bias=eps[:, 0:1], scale=1.0
+            )
+
+        def fin(i, j0, j1):
+            st, mv, sd, rs, nm = sts[i]
+            nc.vector.reciprocal(out=rs[:, j0:j1], in_=sd[:, j0:j1])
+            nc.vector.tensor_scalar(
+                out=nm[:, j0:j1], in0=mv[:, j0:j1, 0], scalar1=-1.0, scalar2=None, op0=ALU.mult
+            )
+
+        def norm(i, j, eng):
+            if j == 0:
+                xn = xnpool.tile([P, JT, D], F32)
+                xns[i] = xn
+            st, mv, sd, rs, nm = sts[i]
+            eng.tensor_scalar(
+                out=xns[i][:, j, :],
+                in0=xts[i][:, j, :],
+                scalar1=nm[:, j : j + 1],
+                scalar2=rs[:, j : j + 1],
+                op0=ALU.add,
+                op1=ALU.mult,
+            )
+
+        def transposes(u):
+            i, g = divmod(u, 2)
+            for t in range(4):
+                kt = 4 * g + t
+                tp = tpsum.tile([P, 512], F32, tag="tp")
+                for j in range(JT):
+                    nc.tensor.transpose(
+                        tp[:, j * P : (j + 1) * P], xns[i][:, j, kt * P : (kt + 1) * P], ident[:]
                     )
-                grp = hpool.tile([P, 512, 4], BF16, align_bytes=64)
-                nc.vector.tensor_copy(
-                    out=grp[:, 0:RV, :].rearrange("p (c i) t -> p c t i", i=4),
-                    in_=hp[:, :, 0:RV].rearrange("p t (c i) -> p c t i", i=4),
+                tps[(u, t)] = tp
+
+        def exits(u):
+            i, g = divmod(u, 2)
+            hp = hpool.tile([P, 4, 512], BF16)
+            grp = hpool.tile([P, 512, 4], BF16, align_bytes=64)
+            hps[u] = hp
+            grps[u] = grp
+            for t in range(4):
+                kt = 4 * g + t
+                nc.scalar.activation(
+                    out=hp[:, t, :],
+                    in_=tps[(u, t)][:],
+                    func=ACTF.Identity,
+                    bias=gbc[:, KT + kt : KT + kt + 1],
+                    scale=gbc[:, kt : kt + 1],
                 )
+
+        def regroup_a(u):
+            rv = rv_cols(u)
+            if rv < 512:
                 nc.scalar.copy(
-                    out=grp[:, RV:512, :].rearrange("p (c i) t -> p c t i", i=4),
-                    in_=hp[:, :, RV:512].rearrange("p t (c i) -> p c t i", i=4),
+                    out=grps[u][:, rv:512, :].rearrange("p (c i) t -> p c t i", i=4),
+                    in_=hps[u][:, :, rv:512].rearrange("p t (c i) -> p c t i", i=4),
                 )
-                nc.vector.quantize_mx(
-                    out=cod[:, g, :].bitcast(FP8X4),
-                    scales=sc[:, g, :],
-                    in_=grp[:].rearrange("p c t -> p (c t)"),
+
+        def regroup_v(u):
+            rv = rv_cols(u)
+            if rv > 0:
+                nc.vector.tensor_copy(
+                    out=grps[u][:, 0:rv, :].rearrange("p (c i) t -> p c t i", i=4),
+                    in_=hps[u][:, :, 0:rv].rearrange("p t (c i) -> p c t i", i=4),
                 )
-            cods[i] = (cod, sc)
+
+        def quant(u):
+            i, g = divmod(u, 2)
+            if g == 0:
+                cod = qpool.tile([P, PASSES, 512], U32, align_bytes=64)
+                sc = qpool.tile([P, PASSES, 512], U8, align_bytes=64)
+                cods[i] = (cod, sc)
+            cod, sc = cods[i]
+            nc.vector.quantize_mx(
+                out=cod[:, g, :].bitcast(FP8X4),
+                scales=sc[:, g, :],
+                in_=grps[u][:].rearrange("p c t -> p (c t)"),
+            )
 
         def project(i):
             cod, sc = cods[i]
-            ot = opool.tile([P, 6, JT, 64], F32)
+            psa = mpsum.tile([P, 512], F32, tag="mm")
+            psb = mpsum.tile([P, 512], F32, tag="mm")
+            psc = mpsum.tile([P, 512], F32, tag="mm")
+            pss[i] = (psa, psb, psc)
             for j in range(JT):
-                ps = mpsum.tile([P, 512], F32, tag="mm")
-                for c0, cw in ((0, 256), (256, 128)):
+                wide = (psa, psb)[j // 2][:, (j % 2) * 256 : (j % 2) * 256 + 256]
+                narrow = psc[:, j * P : (j + 1) * P]
+                for dst, c0, cw in ((wide, 0, 256), (narrow, 256, 128)):
                     for g in range(PASSES):
                         nc.tensor.matmul_mx(
-                            out=ps[:, c0 : c0 + cw],
+                            out=dst,
                             lhsT=cod[:, g, j * P : (j + 1) * P].bitcast(FP8X4),
                             lhsT_scale=sc[:, g, j * P : (j + 1) * P],
                             rhs=wc[:, g * 512 + c0 : g * 512 + c0 + cw].bitcast(FP8X4),
@@ -186,27 +256,122 @@ def tile_vit_transformerblock_pa_t_kernel(
                             start=(g == 0),
                             stop=(g == PASSES - 1),
                         )
+
+        def add_bias(i):
+            ot = opool.tile([P, 6, JT, 64], F32)
+            ots[i] = ot
+            for part in range(2):
                 nc.vector.tensor_tensor(
-                    out=ot[:, :, j, :],
-                    in0=ps[:, 0:NOUT].rearrange("p (c d) -> p c d", d=64),
-                    in1=bias[:].rearrange("p (c d) -> p c d", d=64),
+                    out=ot[:, 0:4, 2 * part : 2 * part + 2, :].rearrange("p c j d -> p j c d"),
+                    in0=pss[i][part][:].rearrange("p (j c d) -> p j c d", j=2, c=4),
+                    in1=bias[:, 0:256].rearrange("p (c d) -> p c d", d=64).unsqueeze(1).to_broadcast([P, 2, 4, 64]),
                     op=ALU.add,
                 )
+            nc.vector.tensor_tensor(
+                out=ot[:, 4:6, :, :].rearrange("p c j d -> p j c d"),
+                in0=pss[i][2][:].rearrange("p (j c d) -> p j c d", j=4, c=2),
+                in1=bias[:, 256:384].rearrange("p (c d) -> p c d", d=64).unsqueeze(1).to_broadcast([P, 4, 2, 64]),
+                op=ALU.add,
+            )
+
+        def store(i):
             b, half = divmod(i, 2)
             for s in range(3):
                 dst = outs[s][b].rearrange("a (h p j) d -> h p a (j d)", h=2, p=P, j=JT)[half]
                 nc.sync.dma_start(
-                    out=dst, in_=ot[:, 2 * s : 2 * s + 2, :, :].rearrange("p a j d -> p a (j d)")
+                    out=dst, in_=ots[i][:, 2 * s : 2 * s + 2, :, :].rearrange("p a j d -> p a (j d)")
                 )
 
-        for i in range(-2, NG + 1):
-            if 0 <= i + 4 < NG and i + 4 >= 2:
-                load(i + 4)
-            if 0 <= i + 2 < NG:
-                stats(i + 2)
-            if 0 <= i + 1 < NG:
-                norm(i + 1)
-            if 0 <= i < NG:
-                quantise(i)
-            if 0 <= i - 1 < NG:
-                project(i - 1)
+        bn(0, 0)
+        bn(0, 1)
+        root(0, 0, 2)
+        bn(0, 2)
+        fin(0, 0, 2)
+        norm(0, 0, nc.gpsimd)
+        norm(0, 1, nc.gpsimd)
+        w_regroup(0)
+        w_regroup(1)
+        bn(0, 3)
+        root(0, 2, 4)
+        prep_gamma()
+        fin(0, 2, 4)
+        norm(0, 2, nc.vector)
+        norm(0, 3, nc.vector)
+        transposes(0)
+        bn(1, 0)
+        bn(1, 1)
+        exits(0)
+        root(1, 0, 2)
+        bn(1, 2)
+        fin(1, 0, 2)
+        norm(1, 0, nc.gpsimd)
+        norm(1, 1, nc.gpsimd)
+        bn(1, 3)
+        transposes(1)
+        regroup_a(0)
+        root(1, 2, 4)
+        bn(2, 0)
+        fin(1, 2, 4)
+        norm(1, 2, nc.gpsimd)
+        norm(1, 3, nc.gpsimd)
+        bias_cast()
+
+        todo = [(i, j) for i in range(2, NG) for j in range(JT) if (i, j) != (2, 0)]
+        want_root = []
+        want_fin = []
+        done = [0, 0, 0]
+
+        def stat():
+            if done[0] < len(todo):
+                i, j = todo[done[0]]
+                done[0] += 1
+                bn(i, j)
+                if j == JT - 1:
+                    want_root.append(i)
+                if j == 0 and loaded[0] < NG:
+                    load(loaded[0], 1)
+                    loaded[0] += 1
+
+        def roots():
+            while done[1] < len(want_root):
+                i = want_root[done[1]]
+                done[1] += 1
+                root(i, 0, JT)
+                want_fin.append(i)
+
+        def finishes():
+            while done[2] < len(want_fin):
+                i = want_fin[done[2]]
+                done[2] += 1
+                fin(i, 0, JT)
+                for j in range(JT):
+                    norm(i, j, nc.gpsimd)
+
+        for a in range(PRE):
+            stat()
+        for n in range(1, NU + 4):
+            if n - 1 < NU:
+                regroup_v(n - 1)
+            stat()
+            finishes()
+            if n - 1 < NU:
+                quant(n - 1)
+            if n + 1 < NU:
+                transposes(n + 1)
+            if n % 2 == 0 and 0 <= (n - 2) // 2 < NG:
+                project((n - 2) // 2)
+            if n < NU:
+                exits(n)
+            roots()
+            if n < NU:
+                regroup_a(n)
+            stat()
+            finishes()
+            if n == 1:
+                w_quant()
+            if n % 2 == 1 and 0 <= (n - 3) // 2 < NG:
+                add_bias((n - 3) // 2)
+                store((n - 3) // 2)
+            if n % EXTRA == 0:
+                stat()
+            roots()

@@ -32,7 +32,7 @@ SWITCH = 22
 RV_EARLY = 0
 RV_LATE = 448
 PRE = 3
-EXTRA = 2
+EXTRA = 3
 
 
 def rv_cols(u):
@@ -48,7 +48,7 @@ def tile_vit_transformerblock_pa_t_kernel(
         const = ctx.enter_context(tc.tile_pool(name="const", bufs=1))
         xpool = ctx.enter_context(tc.tile_pool(name="xpool", bufs=XBUFS))
         small = ctx.enter_context(tc.tile_pool(name="small", bufs=8))
-        xnpool = ctx.enter_context(tc.tile_pool(name="xnpool", bufs=2))
+        xnpool = ctx.enter_context(tc.tile_pool(name="xnpool", bufs=3))
         hpool = ctx.enter_context(tc.tile_pool(name="hpool", bufs=3))
         qpool = ctx.enter_context(tc.tile_pool(name="qpool", bufs=3))
         opool = ctx.enter_context(tc.tile_pool(name="opool", bufs=3))
@@ -288,15 +288,15 @@ def tile_vit_transformerblock_pa_t_kernel(
         bn(0, 2)
         fin(0, 0, 2)
         norm(0, 0, nc.gpsimd)
-        norm(0, 1, nc.gpsimd)
-        w_regroup(0)
-        w_regroup(1)
+        norm(0, 1, nc.vector)
         bn(0, 3)
         root(0, 2, 4)
         prep_gamma()
         fin(0, 2, 4)
         norm(0, 2, nc.vector)
         norm(0, 3, nc.vector)
+        w_regroup(0)
+        w_regroup(1)
         transposes(0)
         bn(1, 0)
         bn(1, 1)
@@ -305,7 +305,7 @@ def tile_vit_transformerblock_pa_t_kernel(
         bn(1, 2)
         fin(1, 0, 2)
         norm(1, 0, nc.gpsimd)
-        norm(1, 1, nc.gpsimd)
+        norm(1, 1, nc.vector)
         bn(1, 3)
         transposes(1)
         regroup_a(0)
@@ -313,7 +313,7 @@ def tile_vit_transformerblock_pa_t_kernel(
         bn(2, 0)
         fin(1, 2, 4)
         norm(1, 2, nc.gpsimd)
-        norm(1, 3, nc.gpsimd)
+        norm(1, 3, nc.vector)
         bias_cast()
 
         todo = [(i, j) for i in range(2, NG) for j in range(JT) if (i, j) != (2, 0)]
@@ -344,7 +344,7 @@ def tile_vit_transformerblock_pa_t_kernel(
                 i = want_fin[done[2]]
                 done[2] += 1
                 fin(i, 0, JT)
-                for j in range(JT):
+                for j in range(JT - 1):
                     norm(i, j, nc.gpsimd)
 
         for a in range(PRE):
@@ -356,6 +356,8 @@ def tile_vit_transformerblock_pa_t_kernel(
             finishes()
             if n - 1 < NU:
                 quant(n - 1)
+            if n % 2 == 0 and 2 <= (n + 2) // 2 < NG:
+                norm((n + 2) // 2, JT - 1, nc.vector)
             if n + 1 < NU:
                 transposes(n + 1)
             if n % 2 == 0 and 0 <= (n - 2) // 2 < NG:

@@ -19,24 +19,15 @@ NOUT = 3 * E
 JT = 4
 GROUP = P * JT
 NG = ROWS // GROUP
-NU = 2 * NG
 KT = D // P
 PASSES = 2
 EPS = 1e-5
 FLOPS = 2 * ROWS * D * NOUT
 
-LOAD_LEAD = 5
-XBUFS = 10
+RG = 128
+RV = 0
+XBUFS = 6
 TPB = 5
-SWITCH = 22
-RV_EARLY = 0
-RV_LATE = 448
-PRE = 3
-EXTRA = 3
-
-
-def rv_cols(u):
-    return RV_EARLY if u < SWITCH else RV_LATE
 
 
 def tile_vit_transformerblock_pa_t_kernel(
@@ -47,56 +38,44 @@ def tile_vit_transformerblock_pa_t_kernel(
     with ExitStack() as ctx:
         const = ctx.enter_context(tc.tile_pool(name="const", bufs=1))
         xpool = ctx.enter_context(tc.tile_pool(name="xpool", bufs=XBUFS))
-        small = ctx.enter_context(tc.tile_pool(name="small", bufs=8))
-        xnpool = ctx.enter_context(tc.tile_pool(name="xnpool", bufs=3))
+        small = ctx.enter_context(tc.tile_pool(name="small", bufs=5))
+        xnpool = ctx.enter_context(tc.tile_pool(name="xnpool", bufs=2))
         hpool = ctx.enter_context(tc.tile_pool(name="hpool", bufs=3))
+        gpool = ctx.enter_context(tc.tile_pool(name="gpool", bufs=2))
         qpool = ctx.enter_context(tc.tile_pool(name="qpool", bufs=3))
         opool = ctx.enter_context(tc.tile_pool(name="opool", bufs=3))
         tpsum = ctx.enter_context(tc.psum_pool(name="tpsum", bufs=TPB))
         mpsum = ctx.enter_context(tc.psum_pool(name="mpsum", bufs=8 - TPB))
-        ctx.enter_context(tc.manual_schedule())
 
-        xg = x.flatten_outer_dims().rearrange("(g p j) k -> g p j k", p=P, j=JT)
+        xg = x.flatten_outer_dims().rearrange("(g p j) k -> g p (j k)", p=P, j=JT)
 
         xts = {}
         sts = {}
-        sds = {}
-        fins = {}
         xns = {}
-        tps = {}
-        hps = {}
-        grps = {}
         cods = {}
-        pss = {}
-        ots = {}
 
-        def load(i, parts):
+        def load(i):
             xt = xpool.tile([P, JT, D], BF16)
-            step = JT // parts
-            for a in range(parts):
-                nc.sync.dma_start(
-                    out=xt[:, a * step : (a + 1) * step, :], in_=xg[i][:, a * step : (a + 1) * step, :]
-                )
+            nc.sync.dma_start(out=xt[:].rearrange("p j k -> p (j k)"), in_=xg[i])
             xts[i] = xt
 
         gb = const.tile([P, P], BF16)
         nc.vector.memset(gb[:], 0.0)
         nc.scalar.dma_start(out=gb[0:KT, :], in_=gamma.rearrange("(c p) -> c p", p=P))
         nc.scalar.dma_start(out=gb[KT : 2 * KT, :], in_=beta.rearrange("(c p) -> c p", p=P))
-        load(0, 4)
-        load(1, 1)
+        load(0)
+        load(1)
         wraw = const.tile([P, KT, NOUT], BF16)
         for s, w in enumerate([Wq, Wk, Wv]):
             nc.sync.dma_start(
                 out=wraw[:, :, s * E : (s + 1) * E],
                 in_=w.rearrange("(c p) n -> p c n", p=P),
             )
-        for i in range(2, LOAD_LEAD):
-            load(i, 1)
+        load(2)
+        load(3)
         bb = const.tile([P, NOUT], BF16)
         for s, b in enumerate([bq, bk, bv]):
             nc.sync.dma_start(out=bb[:, s * E : (s + 1) * E], in_=b.partition_broadcast(P))
-        loaded = [LOAD_LEAD]
 
         ident = const.tile([P, P], F32)
         make_identity(nc, ident[:])
@@ -104,19 +83,13 @@ def tile_vit_transformerblock_pa_t_kernel(
         nc.vector.memset(eps[:], EPS)
         wgrp = const.tile([P, PASSES, 512, 4], BF16, align_bytes=64)
         nc.vector.memset(wgrp[:, :, NOUT:512, :], 0.0)
+        gbf = const.tile([P, P], F32)
+        nc.vector.tensor_copy(out=gbf[:], in_=gb[:])
+        gbp = tpsum.tile([P, 512], F32, tag="tp")
+        nc.tensor.transpose(gbp[:, 0:P], gbf[:], ident[:])
         gbc = const.tile([P, 2 * KT], F32)
-        wc = const.tile([P, PASSES * 512], U32, align_bytes=64)
-        wsc = const.tile([P, PASSES * 512], U8, align_bytes=64)
-        bias = const.tile([P, NOUT], F32)
-
-        def prep_gamma():
-            gbf = const.tile([P, P], F32)
-            nc.vector.tensor_copy(out=gbf[:], in_=gb[:])
-            gbp = tpsum.tile([P, 512], F32, tag="tp")
-            nc.tensor.transpose(gbp[:, 0:P], gbf[:], ident[:])
-            nc.vector.tensor_copy(out=gbc[:], in_=gbp[:, 0 : 2 * KT])
-
-        def w_regroup(g):
+        nc.vector.tensor_copy(out=gbc[:], in_=gbp[:, 0 : 2 * KT])
+        for g in range(PASSES):
             nc.gpsimd.tensor_scalar(
                 out=wgrp[:, g, 0:NOUT, :],
                 in0=wraw[:, 4 * g : 4 * g + 4, :].rearrange("p t n -> p n t"),
@@ -125,123 +98,99 @@ def tile_vit_transformerblock_pa_t_kernel(
                 op0=ALU.mult,
                 op1=ALU.add,
             )
+        wc = const.tile([P, PASSES * 512], U32, align_bytes=64)
+        wsc = const.tile([P, PASSES * 512], U8, align_bytes=64)
+        nc.vector.quantize_mx(
+            out=wc[:].bitcast(FP8X4),
+            scales=wsc[:],
+            in_=wgrp[:].rearrange("p g n t -> p (g n t)"),
+        )
+        bias = const.tile([P, NOUT], F32)
+        nc.gpsimd.tensor_scalar(
+            out=bias[:], in0=bb[:], scalar1=1.0, scalar2=0.0, op0=ALU.mult, op1=ALU.add
+        )
 
-        def bias_cast():
-            nc.gpsimd.tensor_scalar(
-                out=bias[:], in0=bb[:], scalar1=1.0, scalar2=0.0, op0=ALU.mult, op1=ALU.add
-            )
-
-        def w_quant():
-            nc.vector.quantize_mx(
-                out=wc[:].bitcast(FP8X4),
-                scales=wsc[:],
-                in_=wgrp[:].rearrange("p g n t -> p (g n t)"),
-            )
-
-        def bn(i, j):
-            if j == 0:
-                st = small.tile([P, JT, 2, 6], F32)
-                mv = small.tile([P, JT, 2], F32)
-                sd = small.tile([P, JT], F32)
-                rs = small.tile([P, JT], F32)
-                nm = small.tile([P, JT], F32)
-                sts[i] = (st, mv, sd, rs, nm)
-            st = sts[i][0]
-            mv = sts[i][1]
-            for c in range(2):
-                nc.vector.bn_stats(out=st[:, j, c, :], in_=xts[i][:, j, c * 512 : (c + 1) * 512])
-            nc.vector.bn_aggr(out=mv[:, j, :], in_=st[:, j, :, :].rearrange("p c s -> p (c s)"))
-
-        def root(i, j0, j1):
-            mv = sts[i][1]
-            sd = sts[i][2]
+        def stats(i):
+            xt = xts[i]
+            st = small.tile([P, JT, 2, 6], F32)
+            mv = small.tile([P, JT, 2], F32)
+            for j in range(JT):
+                for c in range(2):
+                    nc.vector.bn_stats(out=st[:, j, c, :], in_=xt[:, j, c * 512 : (c + 1) * 512])
+                nc.vector.bn_aggr(out=mv[:, j, :], in_=st[:, j, :, :].rearrange("p c s -> p (c s)"))
+            rs = small.tile([P, JT], F32)
             nc.scalar.activation(
-                out=sd[:, j0:j1], in_=mv[:, j0:j1, 1], func=ACTF.Sqrt, bias=eps[:, 0:1], scale=1.0
+                out=rs[:], in_=mv[:, :, 1], func=ACTF.Abs_reciprocal_sqrt, bias=eps[:, 0:1], scale=1.0
             )
+            nm = small.tile([P, JT], F32)
+            nc.scalar.mul(out=nm[:], in_=mv[:, :, 0], mul=-1.0)
+            sts[i] = (nm, rs)
 
-        def fin(i, j0, j1):
-            st, mv, sd, rs, nm = sts[i]
-            nc.vector.reciprocal(out=rs[:, j0:j1], in_=sd[:, j0:j1])
-            nc.vector.tensor_scalar(
-                out=nm[:, j0:j1], in0=mv[:, j0:j1, 0], scalar1=-1.0, scalar2=None, op0=ALU.mult
-            )
+        def norm(i):
+            nm, rs = sts[i]
+            xn = xnpool.tile([P, JT, D], F32)
+            for j in range(JT):
+                nc.gpsimd.tensor_scalar(
+                    out=xn[:, j, :],
+                    in0=xts[i][:, j, :],
+                    scalar1=nm[:, j : j + 1],
+                    scalar2=rs[:, j : j + 1],
+                    op0=ALU.add,
+                    op1=ALU.mult,
+                )
+            xns[i] = xn
 
-        def norm(i, j, eng):
-            if j == 0:
-                xn = xnpool.tile([P, JT, D], F32)
-                xns[i] = xn
-            st, mv, sd, rs, nm = sts[i]
-            eng.tensor_scalar(
-                out=xns[i][:, j, :],
-                in0=xts[i][:, j, :],
-                scalar1=nm[:, j : j + 1],
-                scalar2=rs[:, j : j + 1],
-                op0=ALU.add,
-                op1=ALU.mult,
-            )
-
-        def transposes(u):
-            i, g = divmod(u, 2)
-            for t in range(4):
-                kt = 4 * g + t
-                tp = tpsum.tile([P, 512], F32, tag="tp")
-                for j in range(JT):
-                    nc.tensor.transpose(
-                        tp[:, j * P : (j + 1) * P], xns[i][:, j, kt * P : (kt + 1) * P], ident[:]
+        def quantise(i):
+            xn = xns[i]
+            grp = gpool.tile([P, PASSES, 512, 4], BF16, align_bytes=64)
+            for g in range(PASSES):
+                hp = hpool.tile([P, 4, 512], BF16)
+                for t in range(4):
+                    kt = 4 * g + t
+                    tp = tpsum.tile([P, 512], F32, tag="tp")
+                    for j in range(JT):
+                        nc.tensor.transpose(
+                            tp[:, j * P : (j + 1) * P], xn[:, j, kt * P : (kt + 1) * P], ident[:]
+                        )
+                    nc.scalar.activation(
+                        out=hp[:, t, :],
+                        in_=tp[:],
+                        func=ACTF.Identity,
+                        bias=gbc[:, KT + kt : KT + kt + 1],
+                        scale=gbc[:, kt : kt + 1],
                     )
-                tps[(u, t)] = tp
-
-        def exits(u):
-            i, g = divmod(u, 2)
-            hp = hpool.tile([P, 4, 512], BF16)
-            grp = hpool.tile([P, 512, 4], BF16, align_bytes=64)
-            hps[u] = hp
-            grps[u] = grp
-            for t in range(4):
-                kt = 4 * g + t
-                nc.scalar.activation(
-                    out=hp[:, t, :],
-                    in_=tps[(u, t)][:],
-                    func=ACTF.Identity,
-                    bias=gbc[:, KT + kt : KT + kt + 1],
-                    scale=gbc[:, kt : kt + 1],
-                )
-
-        def regroup_a(u):
-            rv = rv_cols(u)
-            if rv < 512:
+                if RG > 0:
+                    nc.gpsimd.tensor_scalar(
+                        out=grp[:, g, 0:RG, :].rearrange("p (c i) t -> p c t i", i=4),
+                        in0=hp[:, :, 0:RG].rearrange("p t (c i) -> p c t i", i=4),
+                        scalar1=1.0,
+                        scalar2=0.0,
+                        op0=ALU.mult,
+                        op1=ALU.add,
+                    )
+                if RV > 0:
+                    nc.vector.tensor_copy(
+                        out=grp[:, g, RG : RG + RV, :].rearrange("p (c i) t -> p c t i", i=4),
+                        in_=hp[:, :, RG : RG + RV].rearrange("p t (c i) -> p c t i", i=4),
+                    )
                 nc.scalar.copy(
-                    out=grps[u][:, rv:512, :].rearrange("p (c i) t -> p c t i", i=4),
-                    in_=hps[u][:, :, rv:512].rearrange("p t (c i) -> p c t i", i=4),
+                    out=grp[:, g, RG + RV : 512, :].rearrange("p (c i) t -> p c t i", i=4),
+                    in_=hp[:, :, RG + RV : 512].rearrange("p t (c i) -> p c t i", i=4),
                 )
-
-        def regroup_v(u):
-            rv = rv_cols(u)
-            if rv > 0:
-                nc.vector.tensor_copy(
-                    out=grps[u][:, 0:rv, :].rearrange("p (c i) t -> p c t i", i=4),
-                    in_=hps[u][:, :, 0:rv].rearrange("p t (c i) -> p c t i", i=4),
-                )
-
-        def quant(u):
-            i, g = divmod(u, 2)
-            if g == 0:
-                cod = qpool.tile([P, PASSES, 512], U32, align_bytes=64)
-                sc = qpool.tile([P, PASSES, 512], U8, align_bytes=64)
-                cods[i] = (cod, sc)
-            cod, sc = cods[i]
+            cod = qpool.tile([P, PASSES, 512], U32, align_bytes=64)
+            sc = qpool.tile([P, PASSES, 512], U8, align_bytes=64)
             nc.vector.quantize_mx(
-                out=cod[:, g, :].bitcast(FP8X4),
-                scales=sc[:, g, :],
-                in_=grps[u][:].rearrange("p c t -> p (c t)"),
+                out=cod[:].rearrange("p g c -> p (g c)").bitcast(FP8X4),
+                scales=sc[:].rearrange("p g c -> p (g c)"),
+                in_=grp[:].rearrange("p g c t -> p (g c t)"),
             )
+            cods[i] = (cod, sc)
 
         def project(i):
             cod, sc = cods[i]
             psa = mpsum.tile([P, 512], F32, tag="mm")
             psb = mpsum.tile([P, 512], F32, tag="mm")
             psc = mpsum.tile([P, 512], F32, tag="mm")
-            pss[i] = (psa, psb, psc)
             for j in range(JT):
                 wide = (psa, psb)[j // 2][:, (j % 2) * 256 : (j % 2) * 256 + 256]
                 narrow = psc[:, j * P : (j + 1) * P]
@@ -256,124 +205,35 @@ def tile_vit_transformerblock_pa_t_kernel(
                             start=(g == 0),
                             stop=(g == PASSES - 1),
                         )
-
-        def add_bias(i):
             ot = opool.tile([P, 6, JT, 64], F32)
-            ots[i] = ot
-            for part in range(2):
+            for part, ps in enumerate((psa, psb)):
                 nc.vector.tensor_tensor(
                     out=ot[:, 0:4, 2 * part : 2 * part + 2, :].rearrange("p c j d -> p j c d"),
-                    in0=pss[i][part][:].rearrange("p (j c d) -> p j c d", j=2, c=4),
+                    in0=ps[:].rearrange("p (j c d) -> p j c d", j=2, c=4),
                     in1=bias[:, 0:256].rearrange("p (c d) -> p c d", d=64).unsqueeze(1).to_broadcast([P, 2, 4, 64]),
                     op=ALU.add,
                 )
             nc.vector.tensor_tensor(
                 out=ot[:, 4:6, :, :].rearrange("p c j d -> p j c d"),
-                in0=pss[i][2][:].rearrange("p (j c d) -> p j c d", j=4, c=2),
+                in0=psc[:].rearrange("p (j c d) -> p j c d", j=4, c=2),
                 in1=bias[:, 256:384].rearrange("p (c d) -> p c d", d=64).unsqueeze(1).to_broadcast([P, 4, 2, 64]),
                 op=ALU.add,
             )
-
-        def store(i):
             b, half = divmod(i, 2)
             for s in range(3):
                 dst = outs[s][b].rearrange("a (h p j) d -> h p a (j d)", h=2, p=P, j=JT)[half]
                 nc.sync.dma_start(
-                    out=dst, in_=ots[i][:, 2 * s : 2 * s + 2, :, :].rearrange("p a j d -> p a (j d)")
+                    out=dst, in_=ot[:, 2 * s : 2 * s + 2, :, :].rearrange("p a j d -> p a (j d)")
                 )
 
-        bn(0, 0)
-        bn(0, 1)
-        root(0, 0, 2)
-        bn(0, 2)
-        fin(0, 0, 2)
-        norm(0, 0, nc.gpsimd)
-        norm(0, 1, nc.vector)
-        bn(0, 3)
-        root(0, 2, 4)
-        prep_gamma()
-        fin(0, 2, 4)
-        norm(0, 2, nc.vector)
-        norm(0, 3, nc.vector)
-        w_regroup(0)
-        w_regroup(1)
-        transposes(0)
-        bn(1, 0)
-        bn(1, 1)
-        exits(0)
-        root(1, 0, 2)
-        bn(1, 2)
-        fin(1, 0, 2)
-        norm(1, 0, nc.gpsimd)
-        norm(1, 1, nc.vector)
-        bn(1, 3)
-        transposes(1)
-        regroup_a(0)
-        root(1, 2, 4)
-        bn(2, 0)
-        fin(1, 2, 4)
-        norm(1, 2, nc.gpsimd)
-        norm(1, 3, nc.vector)
-        bias_cast()
-
-        todo = [(i, j) for i in range(2, NG) for j in range(JT) if (i, j) != (2, 0)]
-        want_root = []
-        want_fin = []
-        done = [0, 0, 0]
-
-        def stat():
-            if done[0] < len(todo):
-                i, j = todo[done[0]]
-                done[0] += 1
-                bn(i, j)
-                if j == JT - 1:
-                    want_root.append(i)
-                if j == 0 and loaded[0] < NG:
-                    load(loaded[0], 1)
-                    loaded[0] += 1
-
-        def roots():
-            while done[1] < len(want_root):
-                i = want_root[done[1]]
-                done[1] += 1
-                root(i, 0, JT)
-                want_fin.append(i)
-
-        def finishes():
-            while done[2] < len(want_fin):
-                i = want_fin[done[2]]
-                done[2] += 1
-                fin(i, 0, JT)
-                for j in range(JT - 1):
-                    norm(i, j, nc.gpsimd)
-
-        for a in range(PRE):
-            stat()
-        for n in range(1, NU + 4):
-            if n - 1 < NU:
-                regroup_v(n - 1)
-            stat()
-            finishes()
-            if n - 1 < NU:
-                quant(n - 1)
-            if n % 2 == 0 and 2 <= (n + 2) // 2 < NG:
-                norm((n + 2) // 2, JT - 1, nc.vector)
-            if n + 1 < NU:
-                transposes(n + 1)
-            if n % 2 == 0 and 0 <= (n - 2) // 2 < NG:
-                project((n - 2) // 2)
-            if n < NU:
-                exits(n)
-            roots()
-            if n < NU:
-                regroup_a(n)
-            stat()
-            finishes()
-            if n == 1:
-                w_quant()
-            if n % 2 == 1 and 0 <= (n - 3) // 2 < NG:
-                add_bias((n - 3) // 2)
-                store((n - 3) // 2)
-            if n % EXTRA == 0:
-                stat()
-            roots()
+        for i in range(-2, NG + 1):
+            if 4 <= i + 4 < NG:
+                load(i + 4)
+            if 0 <= i + 2 < NG:
+                stats(i + 2)
+            if 0 <= i + 1 < NG:
+                norm(i + 1)
+            if 0 <= i < NG:
+                quantise(i)
+            if 0 <= i - 1 < NG:
+                project(i - 1)

@@ -13,18 +13,20 @@ ACTF = mybir.ActivationFunctionType
 
 P = 128
 ROWS = 8192
+SEQ = 1024
 D = 1024
 E = 128
 NOUT = 3 * E
-JT = 4
-GROUP = P * JT
-NG = ROWS // GROUP
+JMAX = 4
 KT = D // P
 PASSES = 2
 EPS = 1e-5
 FLOPS = 2 * ROWS * D * NOUT
 
-RG = 128
+SIZES = [1,1,2,4,4,4,4,4,4,4,4,4,4,4,4,4,4,2,1,1]
+assert sum(SIZES) * P == ROWS
+NG = len(SIZES)
+RG = 64
 RV = 0
 XBUFS = 6
 TPB = 5
@@ -35,10 +37,11 @@ def tile_vit_transformerblock_pa_t_kernel(
 ):
     nc = tc.nc
     outs = [out_0, out_1, out_2]
+    starts = [P * sum(SIZES[:i]) for i in range(NG)]
     with ExitStack() as ctx:
         const = ctx.enter_context(tc.tile_pool(name="const", bufs=1))
         xpool = ctx.enter_context(tc.tile_pool(name="xpool", bufs=XBUFS))
-        small = ctx.enter_context(tc.tile_pool(name="small", bufs=5))
+        small = ctx.enter_context(tc.tile_pool(name="small", bufs=6))
         xnpool = ctx.enter_context(tc.tile_pool(name="xnpool", bufs=2))
         hpool = ctx.enter_context(tc.tile_pool(name="hpool", bufs=3))
         gpool = ctx.enter_context(tc.tile_pool(name="gpool", bufs=2))
@@ -47,7 +50,7 @@ def tile_vit_transformerblock_pa_t_kernel(
         tpsum = ctx.enter_context(tc.psum_pool(name="tpsum", bufs=TPB))
         mpsum = ctx.enter_context(tc.psum_pool(name="mpsum", bufs=8 - TPB))
 
-        xg = x.flatten_outer_dims().rearrange("(g p j) k -> g p (j k)", p=P, j=JT)
+        xf = x.flatten_outer_dims()
 
         xts = {}
         sts = {}
@@ -55,24 +58,28 @@ def tile_vit_transformerblock_pa_t_kernel(
         cods = {}
 
         def load(i):
-            xt = xpool.tile([P, JT, D], BF16)
-            nc.sync.dma_start(out=xt[:].rearrange("p j k -> p (j k)"), in_=xg[i])
+            jt = SIZES[i]
+            xt = xpool.tile([P, JMAX, D], BF16)
+            nc.sync.dma_start(
+                out=xt[:, 0:jt, :],
+                in_=xf[starts[i] : starts[i] + P * jt, :].rearrange("(p j) k -> p j k", j=jt),
+            )
             xts[i] = xt
 
         gb = const.tile([P, P], BF16)
         nc.vector.memset(gb[:], 0.0)
         nc.scalar.dma_start(out=gb[0:KT, :], in_=gamma.rearrange("(c p) -> c p", p=P))
         nc.scalar.dma_start(out=gb[KT : 2 * KT, :], in_=beta.rearrange("(c p) -> c p", p=P))
-        load(0)
-        load(1)
+        for i in range(4):
+            load(i)
         wraw = const.tile([P, KT, NOUT], BF16)
         for s, w in enumerate([Wq, Wk, Wv]):
             nc.sync.dma_start(
                 out=wraw[:, :, s * E : (s + 1) * E],
                 in_=w.rearrange("(c p) n -> p c n", p=P),
             )
-        load(2)
-        load(3)
+        for i in range(4, 6):
+            load(i)
         bb = const.tile([P, NOUT], BF16)
         for s, b in enumerate([bq, bk, bv]):
             nc.sync.dma_start(out=bb[:, s * E : (s + 1) * E], in_=b.partition_broadcast(P))
@@ -89,47 +96,50 @@ def tile_vit_transformerblock_pa_t_kernel(
         nc.tensor.transpose(gbp[:, 0:P], gbf[:], ident[:])
         gbc = const.tile([P, 2 * KT], F32)
         nc.vector.tensor_copy(out=gbc[:], in_=gbp[:, 0 : 2 * KT])
-        for g in range(PASSES):
-            nc.gpsimd.tensor_scalar(
-                out=wgrp[:, g, 0:NOUT, :],
-                in0=wraw[:, 4 * g : 4 * g + 4, :].rearrange("p t n -> p n t"),
-                scalar1=1.0,
-                scalar2=0.0,
-                op0=ALU.mult,
-                op1=ALU.add,
-            )
         wc = const.tile([P, PASSES * 512], U32, align_bytes=64)
         wsc = const.tile([P, PASSES * 512], U8, align_bytes=64)
-        nc.vector.quantize_mx(
-            out=wc[:].bitcast(FP8X4),
-            scales=wsc[:],
-            in_=wgrp[:].rearrange("p g n t -> p (g n t)"),
-        )
         bias = const.tile([P, NOUT], F32)
-        nc.gpsimd.tensor_scalar(
-            out=bias[:], in0=bb[:], scalar1=1.0, scalar2=0.0, op0=ALU.mult, op1=ALU.add
-        )
+
+        def prep_w():
+            for g in range(PASSES):
+                nc.gpsimd.tensor_scalar(
+                    out=wgrp[:, g, 0:NOUT, :],
+                    in0=wraw[:, 4 * g : 4 * g + 4, :].rearrange("p t n -> p n t"),
+                    scalar1=1.0,
+                    scalar2=0.0,
+                    op0=ALU.mult,
+                    op1=ALU.add,
+                )
+            nc.vector.quantize_mx(
+                out=wc[:].bitcast(FP8X4),
+                scales=wsc[:],
+                in_=wgrp[:].rearrange("p g n t -> p (g n t)"),
+            )
+            nc.gpsimd.tensor_scalar(
+                out=bias[:], in0=bb[:], scalar1=1.0, scalar2=0.0, op0=ALU.mult, op1=ALU.add
+            )
 
         def stats(i):
+            jt = SIZES[i]
             xt = xts[i]
-            st = small.tile([P, JT, 2, 6], F32)
-            mv = small.tile([P, JT, 2], F32)
-            for j in range(JT):
+            st = small.tile([P, JMAX, 2, 6], F32)
+            mv = small.tile([P, JMAX, 2], F32)
+            for j in range(jt):
                 for c in range(2):
                     nc.vector.bn_stats(out=st[:, j, c, :], in_=xt[:, j, c * 512 : (c + 1) * 512])
                 nc.vector.bn_aggr(out=mv[:, j, :], in_=st[:, j, :, :].rearrange("p c s -> p (c s)"))
-            rs = small.tile([P, JT], F32)
+            rs = small.tile([P, JMAX], F32)
             nc.scalar.activation(
-                out=rs[:], in_=mv[:, :, 1], func=ACTF.Abs_reciprocal_sqrt, bias=eps[:, 0:1], scale=1.0
+                out=rs[:, 0:jt], in_=mv[:, 0:jt, 1], func=ACTF.Abs_reciprocal_sqrt, bias=eps[:, 0:1], scale=1.0
             )
-            nm = small.tile([P, JT], F32)
-            nc.scalar.mul(out=nm[:], in_=mv[:, :, 0], mul=-1.0)
+            nm = small.tile([P, JMAX], F32)
+            nc.scalar.mul(out=nm[:, 0:jt], in_=mv[:, 0:jt, 0], mul=-1.0)
             sts[i] = (nm, rs)
 
         def norm(i):
             nm, rs = sts[i]
-            xn = xnpool.tile([P, JT, D], F32)
-            for j in range(JT):
+            xn = xnpool.tile([P, JMAX, D], F32)
+            for j in range(SIZES[i]):
                 nc.gpsimd.tensor_scalar(
                     out=xn[:, j, :],
                     in0=xts[i][:, j, :],
@@ -140,99 +150,125 @@ def tile_vit_transformerblock_pa_t_kernel(
                 )
             xns[i] = xn
 
+        def regroup(eng_copy, dst, src, c0, c1):
+            eng_copy(
+                dst[:, c0:c1, :].rearrange("p (c i) t -> p c t i", i=4),
+                src[:, :, c0:c1].rearrange("p t (c i) -> p c t i", i=4),
+            )
+
+        def copy_g(out, in_):
+            nc.gpsimd.tensor_scalar(out=out, in0=in_, scalar1=1.0, scalar2=0.0, op0=ALU.mult, op1=ALU.add)
+
+        def copy_v(out, in_):
+            nc.vector.tensor_copy(out=out, in_=in_)
+
+        def copy_a(out, in_):
+            nc.scalar.copy(out=out, in_=in_)
+
         def quantise(i):
+            jt = SIZES[i]
+            w = P * jt
             xn = xns[i]
-            grp = gpool.tile([P, PASSES, 512, 4], BF16, align_bytes=64)
+            flat = gpool.tile([P, PASSES * 512 * 4], BF16, align_bytes=64)
+            grp = flat[:, 0 : PASSES * w * 4].rearrange("p (g c t) -> p g c t", g=PASSES, t=4)
             for g in range(PASSES):
                 hp = hpool.tile([P, 4, 512], BF16)
                 for t in range(4):
                     kt = 4 * g + t
                     tp = tpsum.tile([P, 512], F32, tag="tp")
-                    for j in range(JT):
+                    for j in range(jt):
                         nc.tensor.transpose(
                             tp[:, j * P : (j + 1) * P], xn[:, j, kt * P : (kt + 1) * P], ident[:]
                         )
                     nc.scalar.activation(
-                        out=hp[:, t, :],
-                        in_=tp[:],
+                        out=hp[:, t, 0:w],
+                        in_=tp[:, 0:w],
                         func=ACTF.Identity,
                         bias=gbc[:, KT + kt : KT + kt + 1],
                         scale=gbc[:, kt : kt + 1],
                     )
-                if RG > 0:
-                    nc.gpsimd.tensor_scalar(
-                        out=grp[:, g, 0:RG, :].rearrange("p (c i) t -> p c t i", i=4),
-                        in0=hp[:, :, 0:RG].rearrange("p t (c i) -> p c t i", i=4),
-                        scalar1=1.0,
-                        scalar2=0.0,
-                        op0=ALU.mult,
-                        op1=ALU.add,
-                    )
-                if RV > 0:
-                    nc.vector.tensor_copy(
-                        out=grp[:, g, RG : RG + RV, :].rearrange("p (c i) t -> p c t i", i=4),
-                        in_=hp[:, :, RG : RG + RV].rearrange("p t (c i) -> p c t i", i=4),
-                    )
-                nc.scalar.copy(
-                    out=grp[:, g, RG + RV : 512, :].rearrange("p (c i) t -> p c t i", i=4),
-                    in_=hp[:, :, RG + RV : 512].rearrange("p t (c i) -> p c t i", i=4),
-                )
-            cod = qpool.tile([P, PASSES, 512], U32, align_bytes=64)
-            sc = qpool.tile([P, PASSES, 512], U8, align_bytes=64)
+                rg = RG if jt == JMAX else 0
+                rv = RV if jt == JMAX else 0
+                if rg > 0:
+                    regroup(copy_g, grp[:, g], hp, 0, rg)
+                if rv > 0:
+                    regroup(copy_v, grp[:, g], hp, rg, rg + rv)
+                regroup(copy_a, grp[:, g], hp, rg + rv, w)
+            cod = qpool.tile([P, PASSES * 512], U32, align_bytes=64)
+            sc = qpool.tile([P, PASSES * 512], U8, align_bytes=64)
             nc.vector.quantize_mx(
-                out=cod[:].rearrange("p g c -> p (g c)").bitcast(FP8X4),
-                scales=sc[:].rearrange("p g c -> p (g c)"),
-                in_=grp[:].rearrange("p g c t -> p (g c t)"),
+                out=cod[:, 0 : PASSES * w].bitcast(FP8X4),
+                scales=sc[:, 0 : PASSES * w],
+                in_=flat[:, 0 : PASSES * w * 4],
             )
             cods[i] = (cod, sc)
 
-        def project(i):
+        def passes(i, j, dst, c0, cw):
             cod, sc = cods[i]
-            psa = mpsum.tile([P, 512], F32, tag="mm")
-            psb = mpsum.tile([P, 512], F32, tag="mm")
-            psc = mpsum.tile([P, 512], F32, tag="mm")
-            for j in range(JT):
-                wide = (psa, psb)[j // 2][:, (j % 2) * 256 : (j % 2) * 256 + 256]
-                narrow = psc[:, j * P : (j + 1) * P]
-                for dst, c0, cw in ((wide, 0, 256), (narrow, 256, 128)):
-                    for g in range(PASSES):
-                        nc.tensor.matmul_mx(
-                            out=dst,
-                            lhsT=cod[:, g, j * P : (j + 1) * P].bitcast(FP8X4),
-                            lhsT_scale=sc[:, g, j * P : (j + 1) * P],
-                            rhs=wc[:, g * 512 + c0 : g * 512 + c0 + cw].bitcast(FP8X4),
-                            rhs_scale=wsc[:, g * 512 + c0 : g * 512 + c0 + cw],
-                            start=(g == 0),
-                            stop=(g == PASSES - 1),
-                        )
-            ot = opool.tile([P, 6, JT, 64], F32)
-            for part, ps in enumerate((psa, psb)):
+            w = P * SIZES[i]
+            for g in range(PASSES):
+                a = g * w + j * P
+                nc.tensor.matmul_mx(
+                    out=dst,
+                    lhsT=cod[:, a : a + P].bitcast(FP8X4),
+                    lhsT_scale=sc[:, a : a + P],
+                    rhs=wc[:, g * 512 + c0 : g * 512 + c0 + cw].bitcast(FP8X4),
+                    rhs_scale=wsc[:, g * 512 + c0 : g * 512 + c0 + cw],
+                    start=(g == 0),
+                    stop=(g == PASSES - 1),
+                )
+
+        def project(i):
+            jt = SIZES[i]
+            oflat = opool.tile([P, 6 * JMAX * 64], F32)
+            ot = oflat[:, 0 : 6 * jt * 64].rearrange("p (c j d) -> p c j d", c=6, d=64)
+            if jt == JMAX:
+                psa = mpsum.tile([P, 512], F32, tag="mm")
+                psb = mpsum.tile([P, 512], F32, tag="mm")
+                psc = mpsum.tile([P, 512], F32, tag="mm")
+                for j in range(jt):
+                    passes(i, j, (psa, psb)[j // 2][:, (j % 2) * 256 : (j % 2) * 256 + 256], 0, 256)
+                    passes(i, j, psc[:, j * P : (j + 1) * P], 256, 128)
+                for part, ps in enumerate((psa, psb)):
+                    nc.vector.tensor_tensor(
+                        out=ot[:, 0:4, 2 * part : 2 * part + 2, :].rearrange("p c j d -> p j c d"),
+                        in0=ps[:].rearrange("p (j c d) -> p j c d", j=2, c=4),
+                        in1=bias[:, 0:256].rearrange("p (c d) -> p c d", d=64).unsqueeze(1).to_broadcast([P, 2, 4, 64]),
+                        op=ALU.add,
+                    )
                 nc.vector.tensor_tensor(
-                    out=ot[:, 0:4, 2 * part : 2 * part + 2, :].rearrange("p c j d -> p j c d"),
-                    in0=ps[:].rearrange("p (j c d) -> p j c d", j=2, c=4),
-                    in1=bias[:, 0:256].rearrange("p (c d) -> p c d", d=64).unsqueeze(1).to_broadcast([P, 2, 4, 64]),
+                    out=ot[:, 4:6, :, :].rearrange("p c j d -> p j c d"),
+                    in0=psc[:].rearrange("p (j c d) -> p j c d", j=4, c=2),
+                    in1=bias[:, 256:384].rearrange("p (c d) -> p c d", d=64).unsqueeze(1).to_broadcast([P, 4, 2, 64]),
                     op=ALU.add,
                 )
-            nc.vector.tensor_tensor(
-                out=ot[:, 4:6, :, :].rearrange("p c j d -> p j c d"),
-                in0=psc[:].rearrange("p (j c d) -> p j c d", j=4, c=2),
-                in1=bias[:, 256:384].rearrange("p (c d) -> p c d", d=64).unsqueeze(1).to_broadcast([P, 4, 2, 64]),
-                op=ALU.add,
-            )
-            b, half = divmod(i, 2)
+            else:
+                for j in range(jt):
+                    ps = mpsum.tile([P, 512], F32, tag="mm")
+                    passes(i, j, ps[:, 0:256], 0, 256)
+                    passes(i, j, ps[:, 256:384], 256, 128)
+                    nc.vector.tensor_tensor(
+                        out=ot[:, :, j, :],
+                        in0=ps[:, 0:NOUT].rearrange("p (c d) -> p c d", d=64),
+                        in1=bias[:].rearrange("p (c d) -> p c d", d=64),
+                        op=ALU.add,
+                    )
+            b, n0 = divmod(starts[i], SEQ)
             for s in range(3):
-                dst = outs[s][b].rearrange("a (h p j) d -> h p a (j d)", h=2, p=P, j=JT)[half]
                 nc.sync.dma_start(
-                    out=dst, in_=ot[:, 2 * s : 2 * s + 2, :, :].rearrange("p a j d -> p a (j d)")
+                    out=outs[s][b][:, n0 : n0 + P * jt, :].rearrange("a (p j) d -> p a (j d)", j=jt),
+                    in_=ot[:, 2 * s : 2 * s + 2, :, :].rearrange("p a j d -> p a (j d)"),
                 )
 
         for i in range(-2, NG + 1):
-            if 4 <= i + 4 < NG:
+            if 6 <= i + 4 < NG:
                 load(i + 4)
             if 0 <= i + 2 < NG:
                 stats(i + 2)
             if 0 <= i + 1 < NG:
                 norm(i + 1)
+            if i == 0:
+                prep_w()
             if 0 <= i < NG:
                 quantise(i)
             if 0 <= i - 1 < NG:

@@ -26,7 +26,7 @@ FLOPS = 2 * ROWS * D * NOUT
 SIZES = [1,1,2,4,4,4,4,4,4,4,4,4,4,4,4,4,4,2,1,1]
 assert sum(SIZES) * P == ROWS
 NG = len(SIZES)
-RG = 64
+RG = 192
 RV = 0
 XBUFS = 6
 TPB = 5
@@ -133,7 +133,9 @@ def tile_vit_transformerblock_pa_t_kernel(
                 out=rs[:, 0:jt], in_=mv[:, 0:jt, 1], func=ACTF.Abs_reciprocal_sqrt, bias=eps[:, 0:1], scale=1.0
             )
             nm = small.tile([P, JMAX], F32)
-            nc.scalar.mul(out=nm[:, 0:jt], in_=mv[:, 0:jt, 0], mul=-1.0)
+            nc.gpsimd.tensor_scalar(
+                out=nm[:, 0:jt], in0=mv[:, 0:jt, 0], scalar1=-1.0, scalar2=0.0, op0=ALU.mult, op1=ALU.add
+            )
             sts[i] = (nm, rs)
 
         def norm(i):

@@ -23,11 +23,11 @@ PASSES = 2
 EPS = 1e-5
 FLOPS = 2 * ROWS * D * NOUT
 
-SIZES = [1,1,2,4,4,4,4,4,4,4,4,4,4,4,4,4,4,2,1,1]
+SIZES = [1,1,2,4,4,4,4,4,4,4,4,4,4,4,4,4,4,2,2]
 assert sum(SIZES) * P == ROWS
 NG = len(SIZES)
-RG = 192
-RV = 0
+RG = 64
+RV = 64
 XBUFS = 6
 TPB = 5
 
@@ -133,9 +133,7 @@ def tile_vit_transformerblock_pa_t_kernel(
                 out=rs[:, 0:jt], in_=mv[:, 0:jt, 1], func=ACTF.Abs_reciprocal_sqrt, bias=eps[:, 0:1], scale=1.0
             )
             nm = small.tile([P, JMAX], F32)
-            nc.gpsimd.tensor_scalar(
-                out=nm[:, 0:jt], in0=mv[:, 0:jt, 0], scalar1=-1.0, scalar2=0.0, op0=ALU.mult, op1=ALU.add
-            )
+            nc.scalar.mul(out=nm[:, 0:jt], in_=mv[:, 0:jt, 0], mul=-1.0)
             sts[i] = (nm, rs)
 
         def norm(i):

@@ -189,6 +189,8 @@ def tile_vit_transformerblock_pa_t_kernel(
                     )
                 rg = RG if jt == JMAX else 0
                 rv = RV if jt == JMAX else 0
+                if i >= NG - 4:
+                    rv = 384 if jt == JMAX else 3 * w // 4
                 if rg > 0:
                     regroup(copy_g, grp[:, g], hp, 0, rg)
                 if rv > 0:

from contextlib import ExitStack

import concourse.mybir as mybir
from concourse.masks import make_identity

F32 = mybir.dt.float32
BF16 = mybir.dt.bfloat16
U32 = mybir.dt.uint32
U8 = mybir.dt.uint8
FP8X4 = mybir.dt.float8_e4m3fn_x4
ALU = mybir.AluOpType
ACTF = mybir.ActivationFunctionType

P = 128
ROWS = 8192
SEQ = 1024
D = 1024
E = 128
NOUT = 3 * E
JMAX = 4
KT = D // P
PASSES = 2
EPS = 1e-5
FLOPS = 2 * ROWS * D * NOUT

SIZES = [1,1,2,4,4,4,4,4,4,4,4,4,4,4,4,4,4,2,2]
assert sum(SIZES) * P == ROWS
NG = len(SIZES)
RG = 64
RV = 64
XBUFS = 6
TPB = 5


def tile_vit_transformerblock_pa_t_kernel(
    tc, x, gamma, beta, Wq, bq, Wk, bk, Wv, bv, out_0, out_1, out_2
):
    nc = tc.nc
    outs = [out_0, out_1, out_2]
    starts = [P * sum(SIZES[:i]) for i in range(NG)]
    with ExitStack() as ctx:
        const = ctx.enter_context(tc.tile_pool(name="const", bufs=1))
        xpool = ctx.enter_context(tc.tile_pool(name="xpool", bufs=XBUFS))
        small = ctx.enter_context(tc.tile_pool(name="small", bufs=6))
        xnpool = ctx.enter_context(tc.tile_pool(name="xnpool", bufs=2))
        hpool = ctx.enter_context(tc.tile_pool(name="hpool", bufs=3))
        gpool = ctx.enter_context(tc.tile_pool(name="gpool", bufs=2))
        qpool = ctx.enter_context(tc.tile_pool(name="qpool", bufs=3))
        opool = ctx.enter_context(tc.tile_pool(name="opool", bufs=3))
        tpsum = ctx.enter_context(tc.psum_pool(name="tpsum", bufs=TPB))
        mpsum = ctx.enter_context(tc.psum_pool(name="mpsum", bufs=8 - TPB))

        xf = x.flatten_outer_dims()

        xts = {}
        sts = {}
        xns = {}
        cods = {}

        def load(i):
            jt = SIZES[i]
            xt = xpool.tile([P, JMAX, D], BF16)
            nc.sync.dma_start(
                out=xt[:, 0:jt, :],
                in_=xf[starts[i] : starts[i] + P * jt, :].rearrange("(p j) k -> p j k", j=jt),
            )
            xts[i] = xt

        gb = const.tile([P, P], BF16)
        nc.vector.memset(gb[:], 0.0)
        nc.scalar.dma_start(out=gb[0:KT, :], in_=gamma.rearrange("(c p) -> c p", p=P))
        nc.scalar.dma_start(out=gb[KT : 2 * KT, :], in_=beta.rearrange("(c p) -> c p", p=P))
        for i in range(4):
            load(i)
        wraw = const.tile([P, KT, NOUT], BF16)
        for s, w in enumerate([Wq, Wk, Wv]):
            nc.sync.dma_start(
                out=wraw[:, :, s * E : (s + 1) * E],
                in_=w.rearrange("(c p) n -> p c n", p=P),
            )
        for i in range(4, 6):
            load(i)
        bb = const.tile([P, NOUT], BF16)
        for s, b in enumerate([bq, bk, bv]):
            nc.sync.dma_start(out=bb[:, s * E : (s + 1) * E], in_=b.partition_broadcast(P))

        ident = const.tile([P, P], F32)
        make_identity(nc, ident[:])
        eps = const.tile([P, 1], F32)
        nc.vector.memset(eps[:], EPS)
        wgrp = const.tile([P, PASSES, 512, 4], BF16, align_bytes=64)
        nc.vector.memset(wgrp[:, :, NOUT:512, :], 0.0)
        gbf = const.tile([P, P], F32)
        nc.vector.tensor_copy(out=gbf[:], in_=gb[:])
        gbp = tpsum.tile([P, 512], F32, tag="tp")
        nc.tensor.transpose(gbp[:, 0:P], gbf[:], ident[:])
        gbc = const.tile([P, 2 * KT], F32)
        nc.vector.tensor_copy(out=gbc[:], in_=gbp[:, 0 : 2 * KT])
        wc = const.tile([P, PASSES * 512], U32, align_bytes=64)
        wsc = const.tile([P, PASSES * 512], U8, align_bytes=64)
        bias = const.tile([P, NOUT], F32)

        def prep_w():
            for g in range(PASSES):
                nc.gpsimd.tensor_scalar(
                    out=wgrp[:, g, 0:NOUT, :],
                    in0=wraw[:, 4 * g : 4 * g + 4, :].rearrange("p t n -> p n t"),
                    scalar1=1.0,
                    scalar2=0.0,
                    op0=ALU.mult,
                    op1=ALU.add,
                )
            nc.vector.quantize_mx(
                out=wc[:].bitcast(FP8X4),
                scales=wsc[:],
                in_=wgrp[:].rearrange("p g n t -> p (g n t)"),
            )
            nc.gpsimd.tensor_scalar(
                out=bias[:], in0=bb[:], scalar1=1.0, scalar2=0.0, op0=ALU.mult, op1=ALU.add
            )

        def stats(i):
            jt = SIZES[i]
            xt = xts[i]
            st = small.tile([P, JMAX, 2, 6], F32)
            mv = small.tile([P, JMAX, 2], F32)
            for j in range(jt):
                for c in range(2):
                    nc.vector.bn_stats(out=st[:, j, c, :], in_=xt[:, j, c * 512 : (c + 1) * 512])
                nc.vector.bn_aggr(out=mv[:, j, :], in_=st[:, j, :, :].rearrange("p c s -> p (c s)"))
            rs = small.tile([P, JMAX], F32)
            nc.scalar.activation(
                out=rs[:, 0:jt], in_=mv[:, 0:jt, 1], func=ACTF.Abs_reciprocal_sqrt, bias=eps[:, 0:1], scale=1.0
            )
            nm = small.tile([P, JMAX], F32)
            nc.scalar.mul(out=nm[:, 0:jt], in_=mv[:, 0:jt, 0], mul=-1.0)
            sts[i] = (nm, rs)

        def norm(i):
            nm, rs = sts[i]
            xn = xnpool.tile([P, JMAX, D], F32)
            for j in range(SIZES[i]):
                nc.gpsimd.tensor_scalar(
                    out=xn[:, j, :],
                    in0=xts[i][:, j, :],
                    scalar1=nm[:, j : j + 1],
                    scalar2=rs[:, j : j + 1],
                    op0=ALU.add,
                    op1=ALU.mult,
                )
            xns[i] = xn

        def regroup(eng_copy, dst, src, c0, c1):
            eng_copy(
                dst[:, c0:c1, :].rearrange("p (c i) t -> p c t i", i=4),
                src[:, :, c0:c1].rearrange("p t (c i) -> p c t i", i=4),
            )

        def copy_g(out, in_):
            nc.gpsimd.tensor_scalar(out=out, in0=in_, scalar1=1.0, scalar2=0.0, op0=ALU.mult, op1=ALU.add)

        def copy_v(out, in_):
            nc.vector.tensor_copy(out=out, in_=in_)

        def copy_a(out, in_):
            nc.scalar.copy(out=out, in_=in_)

        def quantise(i):
            jt = SIZES[i]
            w = P * jt
            xn = xns[i]
            flat = gpool.tile([P, PASSES * 512 * 4], BF16, align_bytes=64)
            grp = flat[:, 0 : PASSES * w * 4].rearrange("p (g c t) -> p g c t", g=PASSES, t=4)
            for g in range(PASSES):
                hp = hpool.tile([P, 4, 512], BF16)
                for t in range(4):
                    kt = 4 * g + t
                    tp = tpsum.tile([P, 512], F32, tag="tp")
                    for j in range(jt):
                        nc.tensor.transpose(
                            tp[:, j * P : (j + 1) * P], xn[:, j, kt * P : (kt + 1) * P], ident[:]
                        )
                    nc.scalar.activation(
                        out=hp[:, t, 0:w],
                        in_=tp[:, 0:w],
                        func=ACTF.Identity,
                        bias=gbc[:, KT + kt : KT + kt + 1],
                        scale=gbc[:, kt : kt + 1],
                    )
                rg = RG if jt == JMAX else 0
                rv = RV if jt == JMAX else 0
                if i >= NG - 4:
                    rv = 384 if jt == JMAX else 3 * w // 4
                if rg > 0:
                    regroup(copy_g, grp[:, g], hp, 0, rg)
                if rv > 0:
                    regroup(copy_v, grp[:, g], hp, rg, rg + rv)
                regroup(copy_a, grp[:, g], hp, rg + rv, w)
            cod = qpool.tile([P, PASSES * 512], U32, align_bytes=64)
            sc = qpool.tile([P, PASSES * 512], U8, align_bytes=64)
            nc.vector.quantize_mx(
                out=cod[:, 0 : PASSES * w].bitcast(FP8X4),
                scales=sc[:, 0 : PASSES * w],
                in_=flat[:, 0 : PASSES * w * 4],
            )
            cods[i] = (cod, sc)

        def passes(i, j, dst, c0, cw):
            cod, sc = cods[i]
            w = P * SIZES[i]
            for g in range(PASSES):
                a = g * w + j * P
                nc.tensor.matmul_mx(
                    out=dst,
                    lhsT=cod[:, a : a + P].bitcast(FP8X4),
                    lhsT_scale=sc[:, a : a + P],
                    rhs=wc[:, g * 512 + c0 : g * 512 + c0 + cw].bitcast(FP8X4),
                    rhs_scale=wsc[:, g * 512 + c0 : g * 512 + c0 + cw],
                    start=(g == 0),
                    stop=(g == PASSES - 1),
                )

        def project(i):
            jt = SIZES[i]
            oflat = opool.tile([P, 6 * JMAX * 64], F32)
            ot = oflat[:, 0 : 6 * jt * 64].rearrange("p (c j d) -> p c j d", c=6, d=64)
            if jt == JMAX:
                psa = mpsum.tile([P, 512], F32, tag="mm")
                psb = mpsum.tile([P, 512], F32, tag="mm")
                psc = mpsum.tile([P, 512], F32, tag="mm")
                for j in range(jt):
                    passes(i, j, (psa, psb)[j // 2][:, (j % 2) * 256 : (j % 2) * 256 + 256], 0, 256)
                    passes(i, j, psc[:, j * P : (j + 1) * P], 256, 128)
                for part, ps in enumerate((psa, psb)):
                    nc.vector.tensor_tensor(
                        out=ot[:, 0:4, 2 * part : 2 * part + 2, :].rearrange("p c j d -> p j c d"),
                        in0=ps[:].rearrange("p (j c d) -> p j c d", j=2, c=4),
                        in1=bias[:, 0:256].rearrange("p (c d) -> p c d", d=64).unsqueeze(1).to_broadcast([P, 2, 4, 64]),
                        op=ALU.add,
                    )
                nc.vector.tensor_tensor(
                    out=ot[:, 4:6, :, :].rearrange("p c j d -> p j c d"),
                    in0=psc[:].rearrange("p (j c d) -> p j c d", j=4, c=2),
                    in1=bias[:, 256:384].rearrange("p (c d) -> p c d", d=64).unsqueeze(1).to_broadcast([P, 4, 2, 64]),
                    op=ALU.add,
                )
            else:
                for j in range(jt):
                    ps = mpsum.tile([P, 512], F32, tag="mm")
                    passes(i, j, ps[:, 0:256], 0, 256)
                    passes(i, j, ps[:, 256:384], 256, 128)
                    nc.vector.tensor_tensor(
                        out=ot[:, :, j, :],
                        in0=ps[:, 0:NOUT].rearrange("p (c d) -> p c d", d=64),
                        in1=bias[:].rearrange("p (c d) -> p c d", d=64),
                        op=ALU.add,
                    )
            b, n0 = divmod(starts[i], SEQ)
            for s in range(3):
                nc.sync.dma_start(
                    out=outs[s][b][:, n0 : n0 + P * jt, :].rearrange("a (p j) d -> p a (j d)", j=jt),
                    in_=ot[:, 2 * s : 2 * s + 2, :, :].rearrange("p a j d -> p a (j d)"),
                )

        for i in range(-2, NG + 1):
            if 6 <= i + 4 < NG:
                load(i + 4)
            if 0 <= i + 2 < NG:
                stats(i + 2)
            if 0 <= i + 1 < NG:
                norm(i + 1)
            if i == 0:
                prep_w()
            if 0 <= i < NG:
                quantise(i)
            if 0 <= i - 1 < NG:
                project(i - 1)
